import numpy as np
import ml_dtypes

BF16 = ml_dtypes.bfloat16


def bf(x):
    return np.asarray(x, np.float32).astype(BF16)


def f32(x):
    return np.asarray(x, np.float32)


def f64(x):
    return np.asarray(x).astype(np.float64)


def striped(idx):
    return np.tile(idx.reshape(-1, 16).T, (8, 1))


C, S, N, L, DE, DP, DT = 128, 2048, 1024, 32, 64, 128, 128
EPS = 1e-5


def per_pair(v):
    return np.concatenate([np.repeat(v, L, axis=1), np.tile(v, (1, L))], 0)


def pos_tables():
    pos = np.arange(L, dtype=np.float64)
    half = C // 2
    div = np.exp(np.arange(0.0, half, 2.0) * (-np.log(10000.0) / half))
    ang = pos[None, :] * div[:, None]
    emb = np.concatenate([np.sin(ang), np.cos(ang)], 0)
    sep = np.log(np.abs(pos[:, None] - pos[None, :]) + 1.0).reshape(1, N)
    return per_pair(emb), sep


def setup_inputs():
    pe, sep = pos_tables()
    e = np.random.standard_normal((DE, L))
    return {"base": f32(np.random.standard_normal((C, S))), "templ": f32(1.5 * np.random.standard_normal((N, DT)) + 0.5), "gamma": f32(1.0 + 0.1 * np.random.standard_normal((DT, 1))), "beta": f32(0.1 * np.random.standard_normal((DT, 1))), "w_templ": bf(np.random.standard_normal((DT, C)) / np.sqrt(DT)), "seqpair": bf(per_pair(e)), "w_seq": bf(np.random.standard_normal((DP, C)) / np.sqrt(DP)), "sep": f32(sep), "w_sep": f32(0.3 * np.random.standard_normal((C, 1))), "b": f32(0.1 * np.random.standard_normal((C, 1))), "pe": f32(pe), "offs": striped(np.random.permutation(S)[:N])}


def reference(base, templ, gamma, beta, w_templ, seqpair, w_seq, sep, w_sep, b, pe, offs):
    idx = offs[:16].T.reshape(-1)
    x = f64(templ)
    mu = x.mean(-1, keepdims=True)
    var = np.square(x - mu).mean(-1, keepdims=True)
    t = ((x - mu) / np.sqrt(var + EPS)).T * f64(gamma) + f64(beta)
    proj = f64(w_templ).T @ t + f64(w_seq).T @ f64(seqpair) + f64(w_sep) * f64(sep) + f64(b)
    out = f64(base).copy()
    out[:, idx] = proj + f64(pe)
    return out

@@ -1,0 +1,103 @@
+import concourse.mybir as mybir
+from concourse.masks import make_identity
+
+F32 = mybir.dt.float32
+BF16 = mybir.dt.bfloat16
+U16 = mybir.dt.uint16
+ALU = mybir.AluOpType
+ACT = mybir.ActivationFunctionType
+
+P = 128
+SLOTS = 2048
+PAIRS = 1024
+BLOCKS = PAIRS // P
+BANK = 512
+HALVES = PAIRS // BANK
+BLOCKS_PER_HALF = BANK // P
+EPS = 1e-5
+
+FLOPS = 2 * PAIRS * P * (P + P)
+
+
+def tile_pair_emb_w_templ_kernel(
+    tc, base, templ, gamma, beta, w_templ, seqpair, w_seq, sep, w_sep, b, pe, offs, out
+):
+    nc = tc.nc
+    with (
+        tc.tile_pool(name="held", bufs=1) as held,
+        tc.psum_pool(name="psum", bufs=1) as psum,
+    ):
+        x = held.tile([P, BLOCKS, P], F32, name="x")
+        templ_blocks = templ.rearrange("(k p) d -> k p d", p=P)
+        for k in range(BLOCKS):
+            nc.sync.dma_start(x[:, k, :], templ_blocks[k, :, :])
+        vec_rows = held.tile([4, P], F32, name="vec_rows")
+        for r, vec in enumerate((gamma, beta, w_sep, b)):
+            nc.sync.dma_start(vec_rows[r : r + 1, :], vec.rearrange("c one -> one c"))
+        w_seq_sb = held.tile([P, P], BF16, name="w_seq_sb")
+        nc.sync.dma_start(w_seq_sb[:], w_seq)
+        w_templ_sb = held.tile([P, P], BF16, name="w_templ_sb")
+        nc.sync.dma_start(w_templ_sb[:], w_templ)
+        seqpair_sb = held.tile([P, PAIRS], BF16, name="seqpair_sb")
+        nc.sync.dma_start(seqpair_sb[:], seqpair)
+        sep_all = held.tile([P, PAIRS], F32, name="sep_all")
+        nc.sync.dma_start(sep_all[:], sep[0, :].partition_broadcast(P))
+        pe_sb = held.tile([P, PAIRS], F32, name="pe_sb")
+        nc.sync.dma_start(pe_sb[:], pe)
+        offsets = held.tile([P, PAIRS // 16], U16, name="offsets")
+        nc.sync.dma_start(offsets[:], offs)
+        window = held.tile([P, SLOTS], F32, name="window")
+        nc.sync.dma_start(window[:], base)
+
+        ident = held.tile([P, P], F32, name="ident")
+        make_identity(nc, ident[:])
+        eps = held.tile([P, 1], F32, name="eps")
+        nc.vector.memset(eps[:], EPS)
+
+        vec_ps = psum.tile([P, 4], F32, name="vec_ps")
+        nc.tensor.matmul(vec_ps[:], lhsT=vec_rows[:], rhs=ident[0:4, 0:4], start=True, stop=True)
+        vec_cols = held.tile([P, 4], F32, name="vec_cols")
+        nc.vector.tensor_copy(vec_cols[:], vec_ps[:])
+        gamma_col, beta_col = vec_cols[:, 0:1], vec_cols[:, 1:2]
+        w_sep_col, b_col = vec_cols[:, 2:3], vec_cols[:, 3:4]
+
+        sep_term = held.tile([P, PAIRS], F32, name="sep_term")
+        nc.gpsimd.tensor_scalar(sep_term[:], sep_all[:], w_sep_col, b_col, ALU.mult, ALU.add)
+
+        acc = [psum.tile([P, BANK], F32, name=f"acc{h}") for h in range(HALVES)]
+        for h in range(HALVES):
+            nc.tensor.matmul(
+                acc[h][:], lhsT=w_seq_sb[:], rhs=seqpair_sb[:, h * BANK : (h + 1) * BANK], start=True, stop=False
+            )
+
+        stats = held.tile([P, BLOCKS, 6], F32, name="stats")
+        mean_var = held.tile([P, BLOCKS, 2], F32, name="mean_var")
+        std = held.tile([P, BLOCKS], F32, name="std")
+        rstd = held.tile([P, BLOCKS], F32, name="rstd")
+        shift = held.tile([P, BLOCKS], F32, name="shift")
+        xn = held.tile([P, BLOCKS, P], F32, name="xn")
+        t = held.tile([P, PAIRS], BF16, name="t")
+        proj = held.tile([P, PAIRS], F32, name="proj")
+        for h in range(HALVES):
+            first, last = h * BLOCKS_PER_HALF, (h + 1) * BLOCKS_PER_HALF
+            half = slice(h * BANK, (h + 1) * BANK)
+            for k in range(first, last):
+                nc.vector.bn_stats(stats[:, k, :], x[:, k, :])
+                nc.vector.bn_aggr(mean_var[:, k, :], stats[:, k, :])
+            nc.scalar.activation(std[:, first:last], mean_var[:, first:last, 1], ACT.Sqrt, bias=eps[:])
+            nc.vector.reciprocal(rstd[:, first:last], std[:, first:last])
+            nc.vector.scalar_tensor_tensor(
+                shift[:, first:last], mean_var[:, first:last, 0], -1.0, rstd[:, first:last], ALU.mult, ALU.mult
+            )
+            xn_t = psum.tile([P, BANK], F32, name=f"xn_t{h}")
+            for k in range(first, last):
+                nc.scalar.activation(
+                    xn[:, k, :], x[:, k, :], ACT.Identity, scale=rstd[:, k : k + 1], bias=shift[:, k : k + 1]
+                )
+                nc.tensor.transpose(xn_t[:, (k - first) * P : (k - first + 1) * P], xn[:, k, :], ident[:])
+            nc.scalar.activation(t[:, half], xn_t[:], ACT.Identity, scale=gamma_col, bias=beta_col)
+            nc.tensor.matmul(acc[h][:], lhsT=w_templ_sb[:], rhs=t[:, half], start=False, stop=True)
+            nc.vector.tensor_tensor(proj[:, half], acc[h][:], sep_term[:, half], ALU.add)
+
+        nc.vector.tensor_tensor(window[:].indirect(offsets[:]), proj[:], pe_sb[:], ALU.add)
+        nc.sync.dma_start(out, window[:])

@@ -27,17 +27,25 @@ def tile_pair_emb_w_templ_kernel(
         tc.tile_pool(name="held", bufs=1) as held,
         tc.psum_pool(name="psum", bufs=1) as psum,
     ):
+        ident = held.tile([P, P], F32, name="ident")
+        make_identity(nc, ident[:])
+        eps = held.tile([P, 1], F32, name="eps")
+        nc.vector.memset(eps[:], EPS)
+
         x = held.tile([P, BLOCKS, P], F32, name="x")
-        templ_blocks = templ.rearrange("(k p) d -> k p d", p=P)
-        for k in range(BLOCKS):
-            nc.sync.dma_start(x[:, k, :], templ_blocks[k, :, :])
+        templ_blocks = templ.rearrange("(k p) d -> p k d", p=P)
+        for h in range(HALVES):
+            first, last = h * BLOCKS_PER_HALF, (h + 1) * BLOCKS_PER_HALF
+            nc.sync.dma_start(x[:, first:last, :], templ_blocks[:, first:last, :])
         vec_rows = held.tile([4, P], F32, name="vec_rows")
-        for r, vec in enumerate((gamma, beta, w_sep, b)):
-            nc.sync.dma_start(vec_rows[r : r + 1, :], vec.rearrange("c one -> one c"))
-        w_seq_sb = held.tile([P, P], BF16, name="w_seq_sb")
-        nc.sync.dma_start(w_seq_sb[:], w_seq)
+        nc.sync.dma_start(vec_rows[0:1, :], gamma.rearrange("c one -> one c"))
+        nc.sync.dma_start(vec_rows[1:2, :], beta.rearrange("c one -> one c"))
+        nc.gpsimd.dma_start(vec_rows[2:3, :], w_sep.rearrange("c one -> one c"))
+        nc.gpsimd.dma_start(vec_rows[3:4, :], b.rearrange("c one -> one c"))
         w_templ_sb = held.tile([P, P], BF16, name="w_templ_sb")
         nc.sync.dma_start(w_templ_sb[:], w_templ)
+        w_seq_sb = held.tile([P, P], BF16, name="w_seq_sb")
+        nc.gpsimd.dma_start(w_seq_sb[:], w_seq)
         seqpair_sb = held.tile([P, PAIRS], BF16, name="seqpair_sb")
         nc.sync.dma_start(seqpair_sb[:], seqpair)
         sep_all = held.tile([P, PAIRS], F32, name="sep_all")
@@ -48,11 +56,6 @@ def tile_pair_emb_w_templ_kernel(
         nc.sync.dma_start(offsets[:], offs)
         window = held.tile([P, SLOTS], F32, name="window")
         nc.sync.dma_start(window[:], base)
-
-        ident = held.tile([P, P], F32, name="ident")
-        make_identity(nc, ident[:])
-        eps = held.tile([P, 1], F32, name="eps")
-        nc.vector.memset(eps[:], EPS)
 
         vec_ps = psum.tile([P, 4], F32, name="vec_ps")
         nc.tensor.matmul(vec_ps[:], lhsT=vec_rows[:], rhs=ident[0:4, 0:4], start=True, stop=True)

@@ -32,40 +32,35 @@ def tile_pair_emb_w_templ_kernel(
         eps = held.tile([P, 1], F32, name="eps")
         nc.vector.memset(eps[:], EPS)
 
+        vec_rows = held.tile([4, P], F32, name="vec_rows")
+        for r, vec in enumerate((gamma, beta, w_sep, b)):
+            nc.scalar.dma_start(vec_rows[r : r + 1, :], vec.rearrange("c one -> one c"))
         x = held.tile([P, BLOCKS, P], F32, name="x")
         templ_blocks = templ.rearrange("(k p) d -> p k d", p=P)
         for h in range(HALVES):
             first, last = h * BLOCKS_PER_HALF, (h + 1) * BLOCKS_PER_HALF
             nc.sync.dma_start(x[:, first:last, :], templ_blocks[:, first:last, :])
-        vec_rows = held.tile([4, P], F32, name="vec_rows")
-        nc.sync.dma_start(vec_rows[0:1, :], gamma.rearrange("c one -> one c"))
-        nc.sync.dma_start(vec_rows[1:2, :], beta.rearrange("c one -> one c"))
-        nc.gpsimd.dma_start(vec_rows[2:3, :], w_sep.rearrange("c one -> one c"))
-        nc.gpsimd.dma_start(vec_rows[3:4, :], b.rearrange("c one -> one c"))
-        w_templ_sb = held.tile([P, P], BF16, name="w_templ_sb")
-        nc.sync.dma_start(w_templ_sb[:], w_templ)
         w_seq_sb = held.tile([P, P], BF16, name="w_seq_sb")
-        nc.gpsimd.dma_start(w_seq_sb[:], w_seq)
+        nc.sync.dma_start(w_seq_sb[:], w_seq)
         seqpair_sb = held.tile([P, PAIRS], BF16, name="seqpair_sb")
         nc.sync.dma_start(seqpair_sb[:], seqpair)
+        w_templ_sb = held.tile([P, P], BF16, name="w_templ_sb")
+        nc.sync.dma_start(w_templ_sb[:], w_templ)
         sep_all = held.tile([P, PAIRS], F32, name="sep_all")
         nc.sync.dma_start(sep_all[:], sep[0, :].partition_broadcast(P))
         pe_sb = held.tile([P, PAIRS], F32, name="pe_sb")
         nc.sync.dma_start(pe_sb[:], pe)
-        offsets = held.tile([P, PAIRS // 16], U16, name="offsets")
-        nc.sync.dma_start(offsets[:], offs)
         window = held.tile([P, SLOTS], F32, name="window")
         nc.sync.dma_start(window[:], base)
+        offsets = held.tile([P, PAIRS // 16], U16, name="offsets")
+        nc.sync.dma_start(offsets[:], offs)
 
         vec_ps = psum.tile([P, 4], F32, name="vec_ps")
         nc.tensor.matmul(vec_ps[:], lhsT=vec_rows[:], rhs=ident[0:4, 0:4], start=True, stop=True)
         vec_cols = held.tile([P, 4], F32, name="vec_cols")
-        nc.vector.tensor_copy(vec_cols[:], vec_ps[:])
+        nc.scalar.copy(vec_cols[:], vec_ps[:])
         gamma_col, beta_col = vec_cols[:, 0:1], vec_cols[:, 1:2]
         w_sep_col, b_col = vec_cols[:, 2:3], vec_cols[:, 3:4]
-
-        sep_term = held.tile([P, PAIRS], F32, name="sep_term")
-        nc.gpsimd.tensor_scalar(sep_term[:], sep_all[:], w_sep_col, b_col, ALU.mult, ALU.add)
 
         acc = [psum.tile([P, BANK], F32, name=f"acc{h}") for h in range(HALVES)]
         for h in range(HALVES):
@@ -80,7 +75,6 @@ def tile_pair_emb_w_templ_kernel(
         shift = held.tile([P, BLOCKS], F32, name="shift")
         xn = held.tile([P, BLOCKS, P], F32, name="xn")
         t = held.tile([P, PAIRS], BF16, name="t")
-        proj = held.tile([P, PAIRS], F32, name="proj")
         for h in range(HALVES):
             first, last = h * BLOCKS_PER_HALF, (h + 1) * BLOCKS_PER_HALF
             half = slice(h * BANK, (h + 1) * BANK)
@@ -100,6 +94,12 @@ def tile_pair_emb_w_templ_kernel(
                 nc.tensor.transpose(xn_t[:, (k - first) * P : (k - first + 1) * P], xn[:, k, :], ident[:])
             nc.scalar.activation(t[:, half], xn_t[:], ACT.Identity, scale=gamma_col, bias=beta_col)
             nc.tensor.matmul(acc[h][:], lhsT=w_templ_sb[:], rhs=t[:, half], start=False, stop=True)
+
+        sep_term = held.tile([P, PAIRS], F32, name="sep_term")
+        nc.vector.tensor_scalar(sep_term[:], sep_all[:], w_sep_col, b_col, ALU.mult, ALU.add)
+        proj = held.tile([P, PAIRS], F32, name="proj")
+        for h in range(HALVES):
+            half = slice(h * BANK, (h + 1) * BANK)
             nc.vector.tensor_tensor(proj[:, half], acc[h][:], sep_term[:, half], ALU.add)
 
         nc.vector.tensor_tensor(window[:].indirect(offsets[:]), proj[:], pe_sb[:], ALU.add)

@@ -36,10 +36,10 @@ def tile_pair_emb_w_templ_kernel(
         for r, vec in enumerate((gamma, beta, w_sep, b)):
             nc.scalar.dma_start(vec_rows[r : r + 1, :], vec.rearrange("c one -> one c"))
         x = held.tile([P, BLOCKS, P], F32, name="x")
-        templ_blocks = templ.rearrange("(k p) d -> p k d", p=P)
+        templ_halves = templ.rearrange("(h p i) d -> h p i d", h=HALVES, p=P)
         for h in range(HALVES):
             first, last = h * BLOCKS_PER_HALF, (h + 1) * BLOCKS_PER_HALF
-            nc.sync.dma_start(x[:, first:last, :], templ_blocks[:, first:last, :])
+            nc.sync.dma_start(x[:, first:last, :], templ_halves[h])
         w_seq_sb = held.tile([P, P], BF16, name="w_seq_sb")
         nc.sync.dma_start(w_seq_sb[:], w_seq)
         seqpair_sb = held.tile([P, PAIRS], BF16, name="seqpair_sb")
@@ -92,7 +92,13 @@ def tile_pair_emb_w_templ_kernel(
                     xn[:, k, :], x[:, k, :], ACT.Identity, scale=rstd[:, k : k + 1], bias=shift[:, k : k + 1]
                 )
                 nc.tensor.transpose(xn_t[:, (k - first) * P : (k - first + 1) * P], xn[:, k, :], ident[:])
-            nc.scalar.activation(t[:, half], xn_t[:], ACT.Identity, scale=gamma_col, bias=beta_col)
+            nc.scalar.activation(
+                t[:, half].rearrange("d (p i) -> d p i", i=BLOCKS_PER_HALF),
+                xn_t[:].rearrange("d (i p) -> d p i", i=BLOCKS_PER_HALF),
+                ACT.Identity,
+                scale=gamma_col,
+                bias=beta_col,
+            )
             nc.tensor.matmul(acc[h][:], lhsT=w_templ_sb[:], rhs=t[:, half], start=False, stop=True)
 
         sep_term = held.tile([P, PAIRS], F32, name="sep_term")

@@ -70,9 +70,8 @@ def tile_pair_emb_w_templ_kernel(
 
         stats = held.tile([P, BLOCKS, 6], F32, name="stats")
         mean_var = held.tile([P, BLOCKS, 2], F32, name="mean_var")
-        std = held.tile([P, BLOCKS], F32, name="std")
         rstd = held.tile([P, BLOCKS], F32, name="rstd")
-        shift = held.tile([P, BLOCKS], F32, name="shift")
+        shift = held.tile([P, BLOCKS_PER_HALF], F32, name="shift")
         xn = held.tile([P, BLOCKS, P], F32, name="xn")
         t = held.tile([P, PAIRS], BF16, name="t")
         for h in range(HALVES):
@@ -81,16 +80,21 @@ def tile_pair_emb_w_templ_kernel(
             for k in range(first, last):
                 nc.vector.bn_stats(stats[:, k, :], x[:, k, :])
                 nc.vector.bn_aggr(mean_var[:, k, :], stats[:, k, :])
-            nc.scalar.activation(std[:, first:last], mean_var[:, first:last, 1], ACT.Sqrt, bias=eps[:])
-            nc.vector.reciprocal(rstd[:, first:last], std[:, first:last])
-            nc.vector.scalar_tensor_tensor(
-                shift[:, first:last], mean_var[:, first:last, 0], -1.0, rstd[:, first:last], ALU.mult, ALU.mult
-            )
+            nc.scalar.activation(rstd[:, first:last], mean_var[:, first:last, 1], ACT.Abs_reciprocal_sqrt, bias=eps[:])
+            if h == 0:
+                nc.vector.scalar_tensor_tensor(
+                    shift[:], mean_var[:, first:last, 0], -1.0, rstd[:, first:last], ALU.mult, ALU.mult
+                )
             xn_t = psum.tile([P, BANK], F32, name=f"xn_t{h}")
             for k in range(first, last):
-                nc.scalar.activation(
-                    xn[:, k, :], x[:, k, :], ACT.Identity, scale=rstd[:, k : k + 1], bias=shift[:, k : k + 1]
-                )
+                if h == 0:
+                    nc.scalar.activation(
+                        xn[:, k, :], x[:, k, :], ACT.Identity, scale=rstd[:, k : k + 1], bias=shift[:, k : k + 1]
+                    )
+                else:
+                    nc.vector.tensor_scalar(
+                        xn[:, k, :], x[:, k, :], mean_var[:, k, 0:1], rstd[:, k : k + 1], ALU.subtract, ALU.mult
+                    )
                 nc.tensor.transpose(xn_t[:, (k - first) * P : (k - first + 1) * P], xn[:, k, :], ident[:])
             nc.scalar.activation(
                 t[:, half].rearrange("d (p i) -> d p i", i=BLOCKS_PER_HALF),

@@ -32,9 +32,9 @@ def tile_pair_emb_w_templ_kernel(
         eps = held.tile([P, 1], F32, name="eps")
         nc.vector.memset(eps[:], EPS)
 
-        vec_rows = held.tile([4, P], F32, name="vec_rows")
-        for r, vec in enumerate((gamma, beta, w_sep, b)):
-            nc.scalar.dma_start(vec_rows[r : r + 1, :], vec.rearrange("c one -> one c"))
+        norm_rows = held.tile([2, P], F32, name="norm_rows")
+        for r, vec in enumerate((gamma, beta)):
+            nc.scalar.dma_start(norm_rows[r : r + 1, :], vec.rearrange("c one -> one c"))
         x = held.tile([P, BLOCKS, P], F32, name="x")
         templ_halves = templ.rearrange("(h p i) d -> h p i d", h=HALVES, p=P)
         for h in range(HALVES):
@@ -46,21 +46,25 @@ def tile_pair_emb_w_templ_kernel(
         nc.sync.dma_start(seqpair_sb[:], seqpair)
         w_templ_sb = held.tile([P, P], BF16, name="w_templ_sb")
         nc.sync.dma_start(w_templ_sb[:], w_templ)
-        sep_all = held.tile([P, PAIRS], F32, name="sep_all")
-        nc.sync.dma_start(sep_all[:], sep[0, :].partition_broadcast(P))
         pe_sb = held.tile([P, PAIRS], F32, name="pe_sb")
         nc.sync.dma_start(pe_sb[:], pe)
+        out_rows = held.tile([2, P], F32, name="out_rows")
+        for r, vec in enumerate((w_sep, b)):
+            nc.sync.dma_start(out_rows[r : r + 1, :], vec.rearrange("c one -> one c"))
+        sep_all = held.tile([P, PAIRS], F32, name="sep_all")
+        nc.sync.dma_start(sep_all[:], sep[0, :].partition_broadcast(P))
         window = held.tile([P, SLOTS], F32, name="window")
         nc.sync.dma_start(window[:], base)
         offsets = held.tile([P, PAIRS // 16], U16, name="offsets")
         nc.sync.dma_start(offsets[:], offs)
 
         vec_ps = psum.tile([P, 4], F32, name="vec_ps")
-        nc.tensor.matmul(vec_ps[:], lhsT=vec_rows[:], rhs=ident[0:4, 0:4], start=True, stop=True)
-        vec_cols = held.tile([P, 4], F32, name="vec_cols")
-        nc.scalar.copy(vec_cols[:], vec_ps[:])
-        gamma_col, beta_col = vec_cols[:, 0:1], vec_cols[:, 1:2]
-        w_sep_col, b_col = vec_cols[:, 2:3], vec_cols[:, 3:4]
+        nc.tensor.matmul(vec_ps[:, 0:2], lhsT=norm_rows[:], rhs=ident[0:2, 0:2], start=True, stop=True)
+        norm_cols = held.tile([P, 2], F32, name="norm_cols")
+        nc.scalar.copy(norm_cols[:], vec_ps[:, 0:2])
+        gamma_col, beta_col = norm_cols[:, 0:1], norm_cols[:, 1:2]
+        nc.tensor.matmul(vec_ps[:, 2:4], lhsT=out_rows[:], rhs=ident[0:2, 0:2], start=True, stop=True)
+        w_sep_col, b_col = vec_ps[:, 2:3], vec_ps[:, 3:4]
 
         acc = [psum.tile([P, BANK], F32, name=f"acc{h}") for h in range(HALVES)]
         for h in range(HALVES):

@@ -32,9 +32,10 @@ def tile_pair_emb_w_templ_kernel(
         eps = held.tile([P, 1], F32, name="eps")
         nc.vector.memset(eps[:], EPS)
 
-        norm_rows = held.tile([2, P], F32, name="norm_rows")
+        early_rows = held.tile([2 + BLOCKS, P], F32, name="early_rows")
         for r, vec in enumerate((gamma, beta)):
-            nc.scalar.dma_start(norm_rows[r : r + 1, :], vec.rearrange("c one -> one c"))
+            nc.scalar.dma_start(early_rows[r : r + 1, :], vec.rearrange("c one -> one c"))
+        nc.scalar.dma_start(early_rows[2 : 2 + BLOCKS, :], sep.rearrange("one (k p) -> (one k) p", p=P))
         x = held.tile([P, BLOCKS, P], F32, name="x")
         templ_halves = templ.rearrange("(h p i) d -> h p i d", h=HALVES, p=P)
         for h in range(HALVES):
@@ -51,20 +52,27 @@ def tile_pair_emb_w_templ_kernel(
         out_rows = held.tile([2, P], F32, name="out_rows")
         for r, vec in enumerate((w_sep, b)):
             nc.sync.dma_start(out_rows[r : r + 1, :], vec.rearrange("c one -> one c"))
-        sep_all = held.tile([P, PAIRS], F32, name="sep_all")
-        nc.sync.dma_start(sep_all[:], sep[0, :].partition_broadcast(P))
         window = held.tile([P, SLOTS], F32, name="window")
         nc.sync.dma_start(window[:], base)
         offsets = held.tile([P, PAIRS // 16], U16, name="offsets")
         nc.sync.dma_start(offsets[:], offs)
 
-        vec_ps = psum.tile([P, 4], F32, name="vec_ps")
-        nc.tensor.matmul(vec_ps[:, 0:2], lhsT=norm_rows[:], rhs=ident[0:2, 0:2], start=True, stop=True)
-        norm_cols = held.tile([P, 2], F32, name="norm_cols")
-        nc.scalar.copy(norm_cols[:], vec_ps[:, 0:2])
-        gamma_col, beta_col = norm_cols[:, 0:1], norm_cols[:, 1:2]
-        nc.tensor.matmul(vec_ps[:, 2:4], lhsT=out_rows[:], rhs=ident[0:2, 0:2], start=True, stop=True)
-        w_sep_col, b_col = vec_ps[:, 2:3], vec_ps[:, 3:4]
+        EARLY = 2 + BLOCKS
+        vec_ps = psum.tile([P, EARLY + 2], F32, name="vec_ps")
+        nc.tensor.matmul(vec_ps[:, 0:EARLY], lhsT=early_rows[:], rhs=ident[0:EARLY, 0:EARLY], start=True, stop=True)
+        early_cols = held.tile([P, EARLY], F32, name="early_cols")
+        nc.scalar.copy(early_cols[:], vec_ps[:, 0:EARLY])
+        gamma_col, beta_col = early_cols[:, 0:1], early_cols[:, 1:2]
+        nc.tensor.matmul(vec_ps[:, EARLY : EARLY + 2], lhsT=out_rows[:], rhs=ident[0:2, 0:2], start=True, stop=True)
+        w_sep_col, b_col = vec_ps[:, EARLY : EARLY + 1], vec_ps[:, EARLY + 1 : EARLY + 2]
+
+        sep_ps = [psum.tile([P, BANK], F32, name=f"sep_ps{h}") for h in range(HALVES)]
+        for k in range(BLOCKS):
+            nc.tensor.transpose(
+                sep_ps[k // BLOCKS_PER_HALF][:, (k % BLOCKS_PER_HALF) * P : (k % BLOCKS_PER_HALF + 1) * P],
+                early_cols[:, 2 + k : 3 + k].to_broadcast([P, P]),
+                ident[:],
+            )
 
         acc = [psum.tile([P, BANK], F32, name=f"acc{h}") for h in range(HALVES)]
         for h in range(HALVES):
@@ -110,7 +118,9 @@ def tile_pair_emb_w_templ_kernel(
             nc.tensor.matmul(acc[h][:], lhsT=w_templ_sb[:], rhs=t[:, half], start=False, stop=True)
 
         sep_term = held.tile([P, PAIRS], F32, name="sep_term")
-        nc.vector.tensor_scalar(sep_term[:], sep_all[:], w_sep_col, b_col, ALU.mult, ALU.add)
+        for h in range(HALVES):
+            half = slice(h * BANK, (h + 1) * BANK)
+            nc.vector.tensor_scalar(sep_term[:, half], sep_ps[h][:], w_sep_col, b_col, ALU.mult, ALU.add)
         proj = held.tile([P, PAIRS], F32, name="proj")
         for h in range(HALVES):
             half = slice(h * BANK, (h + 1) * BANK)

@@ -16,6 +16,9 @@ HALVES = PAIRS // BANK
 BLOCKS_PER_HALF = BANK // P
 EPS = 1e-5
 
+PIECES = ((0, 4), (4, 2), (6, 2))
+LAST = len(PIECES) - 1
+
 FLOPS = 2 * PAIRS * P * (P + P)
 
 
@@ -37,10 +40,9 @@ def tile_pair_emb_w_templ_kernel(
             nc.scalar.dma_start(early_rows[r : r + 1, :], vec.rearrange("c one -> one c"))
         nc.scalar.dma_start(early_rows[2 : 2 + BLOCKS, :], sep.rearrange("one (k p) -> (one k) p", p=P))
         x = held.tile([P, BLOCKS, P], F32, name="x")
-        templ_halves = templ.rearrange("(h p i) d -> h p i d", h=HALVES, p=P)
-        for h in range(HALVES):
-            first, last = h * BLOCKS_PER_HALF, (h + 1) * BLOCKS_PER_HALF
-            nc.sync.dma_start(x[:, first:last, :], templ_halves[h])
+        for first, n in PIECES:
+            rows = templ[first * P : (first + n) * P, :]
+            nc.sync.dma_start(x[:, first : first + n, :], rows.rearrange("(p i) d -> p i d", i=n))
         w_seq_sb = held.tile([P, P], BF16, name="w_seq_sb")
         nc.sync.dma_start(w_seq_sb[:], w_seq)
         seqpair_sb = held.tile([P, PAIRS], BF16, name="seqpair_sb")
@@ -49,22 +51,21 @@ def tile_pair_emb_w_templ_kernel(
         nc.sync.dma_start(w_templ_sb[:], w_templ)
         pe_sb = held.tile([P, PAIRS], F32, name="pe_sb")
         nc.sync.dma_start(pe_sb[:], pe)
-        out_rows = held.tile([2, P], F32, name="out_rows")
-        for r, vec in enumerate((w_sep, b)):
-            nc.sync.dma_start(out_rows[r : r + 1, :], vec.rearrange("c one -> one c"))
+        w_sep_col = held.tile([P, 1], F32, name="w_sep_col")
+        nc.sync.dma_start(w_sep_col[:], w_sep)
+        b_col = held.tile([P, 1], F32, name="b_col")
+        nc.sync.dma_start(b_col[:], b)
         window = held.tile([P, SLOTS], F32, name="window")
         nc.sync.dma_start(window[:], base)
         offsets = held.tile([P, PAIRS // 16], U16, name="offsets")
         nc.sync.dma_start(offsets[:], offs)
 
         EARLY = 2 + BLOCKS
-        vec_ps = psum.tile([P, EARLY + 2], F32, name="vec_ps")
-        nc.tensor.matmul(vec_ps[:, 0:EARLY], lhsT=early_rows[:], rhs=ident[0:EARLY, 0:EARLY], start=True, stop=True)
+        vec_ps = psum.tile([P, EARLY], F32, name="vec_ps", tag=f"xn_t{LAST}")
+        nc.tensor.matmul(vec_ps[:], lhsT=early_rows[:], rhs=ident[0:EARLY, 0:EARLY], start=True, stop=True)
         early_cols = held.tile([P, EARLY], F32, name="early_cols")
-        nc.scalar.copy(early_cols[:], vec_ps[:, 0:EARLY])
+        nc.scalar.copy(early_cols[:], vec_ps[:])
         gamma_col, beta_col = early_cols[:, 0:1], early_cols[:, 1:2]
-        nc.tensor.matmul(vec_ps[:, EARLY : EARLY + 2], lhsT=out_rows[:], rhs=ident[0:2, 0:2], start=True, stop=True)
-        w_sep_col, b_col = vec_ps[:, EARLY : EARLY + 1], vec_ps[:, EARLY + 1 : EARLY + 2]
 
         sep_ps = [psum.tile([P, BANK], F32, name=f"sep_ps{h}") for h in range(HALVES)]
         for k in range(BLOCKS):
@@ -74,10 +75,10 @@ def tile_pair_emb_w_templ_kernel(
                 ident[:],
             )
 
-        acc = [psum.tile([P, BANK], F32, name=f"acc{h}") for h in range(HALVES)]
-        for h in range(HALVES):
+        acc = [psum.tile([P, n * P], F32, name=f"acc{m}") for m, (first, n) in enumerate(PIECES)]
+        for m, (first, n) in enumerate(PIECES):
             nc.tensor.matmul(
-                acc[h][:], lhsT=w_seq_sb[:], rhs=seqpair_sb[:, h * BANK : (h + 1) * BANK], start=True, stop=False
+                acc[m][:], lhsT=w_seq_sb[:], rhs=seqpair_sb[:, first * P : (first + n) * P], start=True, stop=False
             )
 
         stats = held.tile([P, BLOCKS, 6], F32, name="stats")
@@ -86,20 +87,21 @@ def tile_pair_emb_w_templ_kernel(
         shift = held.tile([P, BLOCKS_PER_HALF], F32, name="shift")
         xn = held.tile([P, BLOCKS, P], F32, name="xn")
         t = held.tile([P, PAIRS], BF16, name="t")
-        for h in range(HALVES):
-            first, last = h * BLOCKS_PER_HALF, (h + 1) * BLOCKS_PER_HALF
-            half = slice(h * BANK, (h + 1) * BANK)
+        proj = held.tile([P, PAIRS], F32, name="proj")
+        for m, (first, n) in enumerate(PIECES):
+            last = first + n
+            cols = slice(first * P, last * P)
             for k in range(first, last):
                 nc.vector.bn_stats(stats[:, k, :], x[:, k, :])
                 nc.vector.bn_aggr(mean_var[:, k, :], stats[:, k, :])
             nc.scalar.activation(rstd[:, first:last], mean_var[:, first:last, 1], ACT.Abs_reciprocal_sqrt, bias=eps[:])
-            if h == 0:
+            if m == 0:
                 nc.vector.scalar_tensor_tensor(
                     shift[:], mean_var[:, first:last, 0], -1.0, rstd[:, first:last], ALU.mult, ALU.mult
                 )
-            xn_t = psum.tile([P, BANK], F32, name=f"xn_t{h}")
+            xn_t = psum.tile([P, n * P], F32, name=f"xn_t{m}")
             for k in range(first, last):
-                if h == 0:
+                if m == 0:
                     nc.scalar.activation(
                         xn[:, k, :], x[:, k, :], ACT.Identity, scale=rstd[:, k : k + 1], bias=shift[:, k : k + 1]
                     )
@@ -108,23 +110,24 @@ def tile_pair_emb_w_templ_kernel(
                         xn[:, k, :], x[:, k, :], mean_var[:, k, 0:1], rstd[:, k : k + 1], ALU.subtract, ALU.mult
                     )
                 nc.tensor.transpose(xn_t[:, (k - first) * P : (k - first + 1) * P], xn[:, k, :], ident[:])
-            nc.scalar.activation(
-                t[:, half].rearrange("d (p i) -> d p i", i=BLOCKS_PER_HALF),
-                xn_t[:].rearrange("d (i p) -> d p i", i=BLOCKS_PER_HALF),
-                ACT.Identity,
-                scale=gamma_col,
-                bias=beta_col,
+            t_piece = t[:, cols].rearrange("d (p i) -> d p i", i=n)
+            turned = xn_t[:].rearrange("d (i p) -> d p i", i=n)
+            if m == LAST:
+                nc.vector.tensor_scalar(t_piece, turned, gamma_col, beta_col, ALU.mult, ALU.add)
+            else:
+                nc.scalar.activation(t_piece, turned, ACT.Identity, scale=gamma_col, bias=beta_col)
+            nc.tensor.matmul(acc[m][:], lhsT=w_templ_sb[:], rhs=t[:, cols], start=False, stop=True)
+            if m == LAST:
+                nc.vector.tensor_scalar_add(proj[:, cols], acc[m][:], b_col[:])
+            else:
+                nc.scalar.activation(proj[:, cols], acc[m][:], ACT.Identity, bias=b_col[:])
+
+        addend = held.tile([P, PAIRS], F32, name="addend")
+        for h in range(HALVES):
+            half = slice(h * BANK, (h + 1) * BANK)
+            nc.vector.scalar_tensor_tensor(
+                addend[:, half], sep_ps[h][:], w_sep_col[:], pe_sb[:, half], ALU.mult, ALU.add
             )
-            nc.tensor.matmul(acc[h][:], lhsT=w_templ_sb[:], rhs=t[:, half], start=False, stop=True)
 
-        sep_term = held.tile([P, PAIRS], F32, name="sep_term")
-        for h in range(HALVES):
-            half = slice(h * BANK, (h + 1) * BANK)
-            nc.vector.tensor_scalar(sep_term[:, half], sep_ps[h][:], w_sep_col, b_col, ALU.mult, ALU.add)
-        proj = held.tile([P, PAIRS], F32, name="proj")
-        for h in range(HALVES):
-            half = slice(h * BANK, (h + 1) * BANK)
-            nc.vector.tensor_tensor(proj[:, half], acc[h][:], sep_term[:, half], ALU.add)
-
-        nc.vector.tensor_tensor(window[:].indirect(offsets[:]), proj[:], pe_sb[:], ALU.add)
+        nc.vector.tensor_tensor(window[:].indirect(offsets[:]), proj[:], addend[:], ALU.add)
         nc.sync.dma_start(out, window[:])

@@ -16,7 +16,7 @@ HALVES = PAIRS // BANK
 BLOCKS_PER_HALF = BANK // P
 EPS = 1e-5
 
-PIECES = ((0, 4), (4, 2), (6, 2))
+PIECES = ((0, 2), (2, 4), (6, 2))
 LAST = len(PIECES) - 1
 
 FLOPS = 2 * PAIRS * P * (P + P)
@@ -40,13 +40,14 @@ def tile_pair_emb_w_templ_kernel(
             nc.scalar.dma_start(early_rows[r : r + 1, :], vec.rearrange("c one -> one c"))
         nc.scalar.dma_start(early_rows[2 : 2 + BLOCKS, :], sep.rearrange("one (k p) -> (one k) p", p=P))
         x = held.tile([P, BLOCKS, P], F32, name="x")
-        for first, n in PIECES:
+        w_seq_sb = held.tile([P, P], BF16, name="w_seq_sb")
+        seqpair_sb = held.tile([P, PAIRS], BF16, name="seqpair_sb")
+        for m, (first, n) in enumerate(PIECES):
+            if m == LAST:
+                nc.sync.dma_start(w_seq_sb[:], w_seq)
+                nc.sync.dma_start(seqpair_sb[:], seqpair)
             rows = templ[first * P : (first + n) * P, :]
             nc.sync.dma_start(x[:, first : first + n, :], rows.rearrange("(p i) d -> p i d", i=n))
-        w_seq_sb = held.tile([P, P], BF16, name="w_seq_sb")
-        nc.sync.dma_start(w_seq_sb[:], w_seq)
-        seqpair_sb = held.tile([P, PAIRS], BF16, name="seqpair_sb")
-        nc.sync.dma_start(seqpair_sb[:], seqpair)
         w_templ_sb = held.tile([P, P], BF16, name="w_templ_sb")
         nc.sync.dma_start(w_templ_sb[:], w_templ)
         pe_sb = held.tile([P, PAIRS], F32, name="pe_sb")
@@ -84,7 +85,7 @@ def tile_pair_emb_w_templ_kernel(
         stats = held.tile([P, BLOCKS, 6], F32, name="stats")
         mean_var = held.tile([P, BLOCKS, 2], F32, name="mean_var")
         rstd = held.tile([P, BLOCKS], F32, name="rstd")
-        shift = held.tile([P, BLOCKS_PER_HALF], F32, name="shift")
+        shift = held.tile([P, BLOCKS], F32, name="shift")
         xn = held.tile([P, BLOCKS, P], F32, name="xn")
         t = held.tile([P, PAIRS], BF16, name="t")
         proj = held.tile([P, PAIRS], F32, name="proj")
@@ -95,13 +96,13 @@ def tile_pair_emb_w_templ_kernel(
                 nc.vector.bn_stats(stats[:, k, :], x[:, k, :])
                 nc.vector.bn_aggr(mean_var[:, k, :], stats[:, k, :])
             nc.scalar.activation(rstd[:, first:last], mean_var[:, first:last, 1], ACT.Abs_reciprocal_sqrt, bias=eps[:])
-            if m == 0:
+            if m < LAST:
                 nc.vector.scalar_tensor_tensor(
-                    shift[:], mean_var[:, first:last, 0], -1.0, rstd[:, first:last], ALU.mult, ALU.mult
+                    shift[:, first:last], mean_var[:, first:last, 0], -1.0, rstd[:, first:last], ALU.mult, ALU.mult
                 )
             xn_t = psum.tile([P, n * P], F32, name=f"xn_t{m}")
             for k in range(first, last):
-                if m == 0:
+                if m < LAST:
                     nc.scalar.activation(
                         xn[:, k, :], x[:, k, :], ACT.Identity, scale=rstd[:, k : k + 1], bias=shift[:, k : k + 1]
                     )

import concourse.mybir as mybir
from concourse.masks import make_identity

F32 = mybir.dt.float32
BF16 = mybir.dt.bfloat16
U16 = mybir.dt.uint16
ALU = mybir.AluOpType
ACT = mybir.ActivationFunctionType

P = 128
SLOTS = 2048
PAIRS = 1024
BLOCKS = PAIRS // P
BANK = 512
HALVES = PAIRS // BANK
BLOCKS_PER_HALF = BANK // P
EPS = 1e-5

PIECES = ((0, 2), (2, 4), (6, 2))
LAST = len(PIECES) - 1

FLOPS = 2 * PAIRS * P * (P + P)


def tile_pair_emb_w_templ_kernel(
    tc, base, templ, gamma, beta, w_templ, seqpair, w_seq, sep, w_sep, b, pe, offs, out
):
    nc = tc.nc
    with (
        tc.tile_pool(name="held", bufs=1) as held,
        tc.psum_pool(name="psum", bufs=1) as psum,
    ):
        ident = held.tile([P, P], F32, name="ident")
        make_identity(nc, ident[:])
        eps = held.tile([P, 1], F32, name="eps")
        nc.vector.memset(eps[:], EPS)

        early_rows = held.tile([2 + BLOCKS, P], F32, name="early_rows")
        for r, vec in enumerate((gamma, beta)):
            nc.scalar.dma_start(early_rows[r : r + 1, :], vec.rearrange("c one -> one c"))
        nc.scalar.dma_start(early_rows[2 : 2 + BLOCKS, :], sep.rearrange("one (k p) -> (one k) p", p=P))
        x = held.tile([P, BLOCKS, P], F32, name="x")
        w_seq_sb = held.tile([P, P], BF16, name="w_seq_sb")
        seqpair_sb = held.tile([P, PAIRS], BF16, name="seqpair_sb")
        for m, (first, n) in enumerate(PIECES):
            if m == LAST:
                nc.sync.dma_start(w_seq_sb[:], w_seq)
                nc.sync.dma_start(seqpair_sb[:], seqpair)
            rows = templ[first * P : (first + n) * P, :]
            nc.sync.dma_start(x[:, first : first + n, :], rows.rearrange("(p i) d -> p i d", i=n))
        w_templ_sb = held.tile([P, P], BF16, name="w_templ_sb")
        nc.sync.dma_start(w_templ_sb[:], w_templ)
        pe_sb = held.tile([P, PAIRS], F32, name="pe_sb")
        nc.sync.dma_start(pe_sb[:], pe)
        w_sep_col = held.tile([P, 1], F32, name="w_sep_col")
        nc.sync.dma_start(w_sep_col[:], w_sep)
        b_col = held.tile([P, 1], F32, name="b_col")
        nc.sync.dma_start(b_col[:], b)
        window = held.tile([P, SLOTS], F32, name="window")
        nc.sync.dma_start(window[:], base)
        offsets = held.tile([P, PAIRS // 16], U16, name="offsets")
        nc.sync.dma_start(offsets[:], offs)

        EARLY = 2 + BLOCKS
        vec_ps = psum.tile([P, EARLY], F32, name="vec_ps", tag=f"xn_t{LAST}")
        nc.tensor.matmul(vec_ps[:], lhsT=early_rows[:], rhs=ident[0:EARLY, 0:EARLY], start=True, stop=True)
        early_cols = held.tile([P, EARLY], F32, name="early_cols")
        nc.scalar.copy(early_cols[:], vec_ps[:])
        gamma_col, beta_col = early_cols[:, 0:1], early_cols[:, 1:2]

        sep_ps = [psum.tile([P, BANK], F32, name=f"sep_ps{h}") for h in range(HALVES)]
        for k in range(BLOCKS):
            nc.tensor.transpose(
                sep_ps[k // BLOCKS_PER_HALF][:, (k % BLOCKS_PER_HALF) * P : (k % BLOCKS_PER_HALF + 1) * P],
                early_cols[:, 2 + k : 3 + k].to_broadcast([P, P]),
                ident[:],
            )

        acc = [psum.tile([P, n * P], F32, name=f"acc{m}") for m, (first, n) in enumerate(PIECES)]
        for m, (first, n) in enumerate(PIECES):
            nc.tensor.matmul(
                acc[m][:], lhsT=w_seq_sb[:], rhs=seqpair_sb[:, first * P : (first + n) * P], start=True, stop=False
            )

        stats = held.tile([P, BLOCKS, 6], F32, name="stats")
        mean_var = held.tile([P, BLOCKS, 2], F32, name="mean_var")
        rstd = held.tile([P, BLOCKS], F32, name="rstd")
        shift = held.tile([P, BLOCKS], F32, name="shift")
        xn = held.tile([P, BLOCKS, P], F32, name="xn")
        t = held.tile([P, PAIRS], BF16, name="t")
        proj = held.tile([P, PAIRS], F32, name="proj")
        for m, (first, n) in enumerate(PIECES):
            last = first + n
            cols = slice(first * P, last * P)
            for k in range(first, last):
                nc.vector.bn_stats(stats[:, k, :], x[:, k, :])
                nc.vector.bn_aggr(mean_var[:, k, :], stats[:, k, :])
            nc.scalar.activation(rstd[:, first:last], mean_var[:, first:last, 1], ACT.Abs_reciprocal_sqrt, bias=eps[:])
            if m < LAST:
                nc.vector.scalar_tensor_tensor(
                    shift[:, first:last], mean_var[:, first:last, 0], -1.0, rstd[:, first:last], ALU.mult, ALU.mult
                )
            xn_t = psum.tile([P, n * P], F32, name=f"xn_t{m}")
            for k in range(first, last):
                if m < LAST:
                    nc.scalar.activation(
                        xn[:, k, :], x[:, k, :], ACT.Identity, scale=rstd[:, k : k + 1], bias=shift[:, k : k + 1]
                    )
                else:
                    nc.vector.tensor_scalar(
                        xn[:, k, :], x[:, k, :], mean_var[:, k, 0:1], rstd[:, k : k + 1], ALU.subtract, ALU.mult
                    )
                nc.tensor.transpose(xn_t[:, (k - first) * P : (k - first + 1) * P], xn[:, k, :], ident[:])
            t_piece = t[:, cols].rearrange("d (p i) -> d p i", i=n)
            turned = xn_t[:].rearrange("d (i p) -> d p i", i=n)
            if m == LAST:
                nc.vector.tensor_scalar(t_piece, turned, gamma_col, beta_col, ALU.mult, ALU.add)
            else:
                nc.scalar.activation(t_piece, turned, ACT.Identity, scale=gamma_col, bias=beta_col)
            nc.tensor.matmul(acc[m][:], lhsT=w_templ_sb[:], rhs=t[:, cols], start=False, stop=True)
            if m == LAST:
                nc.vector.tensor_scalar_add(proj[:, cols], acc[m][:], b_col[:])
            else:
                nc.scalar.activation(proj[:, cols], acc[m][:], ACT.Identity, bias=b_col[:])

        addend = held.tile([P, PAIRS], F32, name="addend")
        for h in range(HALVES):
            half = slice(h * BANK, (h + 1) * BANK)
            nc.vector.scalar_tensor_tensor(
                addend[:, half], sep_ps[h][:], w_sep_col[:], pe_sb[:, half], ALU.mult, ALU.add
            )

        nc.vector.tensor_tensor(window[:].indirect(offsets[:]), proj[:], addend[:], ALU.add)
        nc.sync.dma_start(out, window[:])
